import numpy as np
import ml_dtypes


def mxq(x, axis, fmt="e4m3"):
    dtype, down = {"e4m3": (ml_dtypes.float8_e4m3fn, 7), "e5m2": (ml_dtypes.float8_e5m2, 14)}[fmt]
    v = np.moveaxis(np.asarray(x, np.float32).astype(ml_dtypes.bfloat16).astype(np.float64), axis, -1)
    blocks = v.reshape(v.shape[:-1] + (-1, 32))
    amax = np.abs(blocks).max(-1, keepdims=True)
    byte = np.maximum(np.where(amax > 0, np.frexp(amax)[1] - 1 + 127, 0) - down, 1)
    scale = np.exp2(byte - 127.0)
    codes = (blocks / scale).astype(np.float32).astype(dtype).astype(np.float64)
    return np.moveaxis((codes * scale).reshape(v.shape), -1, axis)


WIDE = False


def mx_kscale(k):
    if not WIDE:
        return np.ones(k)
    levels = np.array([10, -10, 5, -5, 0])
    a = np.random.permutation(np.resize(levels, k // 512 * 4)).reshape(k // 512, 4)
    idx = np.arange(k)
    return np.exp2(a[idx // 512, idx % 128 // 32])


BF16 = ml_dtypes.bfloat16


def bf(x):
    return np.asarray(x, np.float32).astype(BF16)


def f64(x):
    return np.asarray(x).astype(np.float64)


B, D, DO, H, T, P = 8192, 512, 1024, 256, 8, 2


def setup_inputs():
    s = mx_kscale(D)
    return {"transformed": bf(np.random.standard_normal((B, D)) * 1.2 * s),
            "coeff": bf(np.random.standard_normal((B, P)) * 0.45),
            "task_mats": bf(np.random.standard_normal((P, D, D)) / np.sqrt(D) / s[None, :, None] * s[None, None, :])}


def reference(transformed, coeff, task_mats):
    x, c, m = f64(transformed), f64(coeff), f64(task_mats)
    for j in range(P):
        x = x + c[:, j:j + 1] * (mxq(x, 1, "e4m3") @ mxq(m[j], 0, "e4m3"))
    return x

@@ -1,0 +1,207 @@
+from contextlib import ExitStack
+
+import concourse.mybir as mybir
+from concourse.masks import make_identity
+
+F32 = mybir.dt.float32
+BF16 = mybir.dt.bfloat16
+U32 = mybir.dt.uint32
+U8 = mybir.dt.uint8
+FP8X4 = mybir.dt.float8_e4m3fn_x4
+MULT = mybir.AluOpType.mult
+ADD = mybir.AluOpType.add
+
+P = 128
+B = 8192
+D = 512
+NT = B // P
+NP = NT // 2
+FLOPS = 2 * 2 * B * D * D
+
+CHUNKS = [2, 2, 4, 8, 8, 8, 8, 8, 8, 8]
+
+
+def tile_precomputedmetanet_pa_t_kernel(tc, transformed, coeff, task_mats, out):
+    nc = tc.nc
+    x_dram = transformed.rearrange("(p i) d -> p (i d)", i=NT)
+    o_dram = out.rearrange("(p i) d -> p (i d)", i=NT)
+    c_dram = coeff.rearrange("(p i) c -> p (i c)", i=NT)
+
+    with ExitStack() as ctx:
+        const = ctx.enter_context(tc.tile_pool(name="const", bufs=1))
+        gpool = ctx.enter_context(tc.tile_pool(name="gpool", bufs=3))
+        qpool = ctx.enter_context(tc.tile_pool(name="qpool", bufs=3))
+        x1pool = ctx.enter_context(tc.tile_pool(name="x1pool", bufs=6))
+        opool = ctx.enter_context(tc.tile_pool(name="opool", bufs=6))
+        ps_x = ctx.enter_context(tc.psum_pool(name="ps_x", bufs=2))
+        ps_t = ctx.enter_context(tc.psum_pool(name="ps_t", bufs=2))
+        ps_y = ctx.enter_context(tc.psum_pool(name="ps_y", bufs=2))
+        ps_z = ctx.enter_context(tc.psum_pool(name="ps_z", bufs=2))
+        ctx.enter_context(tc.manual_schedule())
+
+        ident = const.tile([P, P], F32, name="ident")
+        make_identity(nc, ident[:])
+
+        w0r = const.tile([P, 4, D], BF16, name="w0r")
+        nc.sync.dma_start(
+            out=w0r[:].rearrange("p (u e) n -> p u (e n)", u=2),
+            in_=task_mats[0].rearrange("(u q e) n -> q u (e n)", u=2, e=2),
+        )
+        xs = []
+        where = {}
+        start = 0
+        w1r = const.tile([P, 4, D], BF16, name="w1r")
+        c_bf = const.tile([P, 2 * NT], BF16, name="c_bf")
+        for c, n in enumerate(CHUNKS):
+            xc = const.tile([P, n * D], BF16, name="x%d" % c)
+            nc.sync.dma_start(out=xc[:], in_=x_dram[:, start * D : (start + n) * D])
+            xs.append(xc)
+            for k in range(n):
+                where[start + k] = (c, k)
+            start += n
+            if c == 0:
+                nc.sync.dma_start(out=c_bf[:], in_=c_dram)
+            if c == 1:
+                nc.sync.dma_start(out=w1r[:], in_=task_mats[1].rearrange("(t p) n -> p t n", t=4))
+        assert start == NT
+
+        def x_bf(i):
+            c, k = where[i]
+            return xs[c][:, k * D : (k + 1) * D]
+
+        def x_words(i, u):
+            c, k = where[i]
+            lo = k * (D // 2) + u * P
+            return xs[c][:].bitcast(F32)[:, lo : lo + P]
+
+        w0g = const.tile([P, D, 4], BF16, name="w0g", align_bytes=64)
+        w0c = const.tile([P, D], U32, name="w0c", align_bytes=64)
+        w0s = const.tile([P, D], U8, name="w0s", align_bytes=64)
+        w1g = const.tile([P, D, 4], BF16, name="w1g", align_bytes=64)
+        w1c = const.tile([P, D], U32, name="w1c", align_bytes=64)
+        w1s = const.tile([P, D], U8, name="w1s", align_bytes=64)
+        c32 = const.tile([P, 2 * NT], F32, name="c32")
+
+        nc.vector.tensor_copy(out=w0g[:], in_=w0r[:].rearrange("p t n -> p n t"))
+        nc.vector.tensor_copy(out=c32[:], in_=c_bf[:])
+        nc.vector.quantize_mx(
+            out=w0c[:].bitcast(FP8X4), scales=w0s[:], in_=w0g[:].rearrange("p n t -> p (n t)")
+        )
+
+        TPX = {}
+        GX = {}
+        QX = {}
+        Y = {}
+        X1 = {}
+        T1 = {}
+        G1 = {}
+        Q1 = {}
+        Z = {}
+
+        def tx(g):
+            t = ps_x.tile([P, 2, 2, P], F32, name="tpx", tag="tpx")
+            for j in range(2):
+                for u in range(2):
+                    nc.tensor.transpose(t[:, j, u, :], x_words(2 * g + j, u), ident[:])
+            TPX[g] = t
+
+        def ex(g):
+            gx = gpool.tile([P, 8 * P], BF16, name="gx", tag="gx", align_bytes=64)
+            nc.scalar.copy(
+                out=gx[:].bitcast(F32).rearrange("p (j k u) -> p j k u", j=2, u=2),
+                in_=TPX[g][:].rearrange("p j u k -> p j k u"),
+            )
+            GX[g] = gx
+
+        def quant(src, tagc, tags):
+            cw = qpool.tile([P, 2 * P], U32, name=tagc, tag=tagc, align_bytes=64)
+            sc = qpool.tile([P, 2 * P], U8, name=tags, tag=tags, align_bytes=64)
+            nc.vector.quantize_mx(out=cw[:].bitcast(FP8X4), scales=sc[:], in_=src[:])
+            return (cw, sc)
+
+        def mm(pool, tag, q, wc, ws):
+            res = []
+            cw, sc = q
+            for j in range(2):
+                acc = pool.tile([P, D], F32, name=tag, tag=tag)
+                nc.tensor.matmul_mx(
+                    out=acc[:],
+                    lhsT=cw[:, j * P : (j + 1) * P].bitcast(FP8X4),
+                    lhsT_scale=sc[:, j * P : (j + 1) * P],
+                    rhs=wc[:].bitcast(FP8X4),
+                    rhs_scale=ws[:],
+                    start=True,
+                    stop=True,
+                )
+                res.append(acc)
+            return res
+
+        def a1(g):
+            x1 = x1pool.tile([P, 2, D], F32, name="x1", tag="x1")
+            for j in range(2):
+                i = 2 * g + j
+                nc.vector.scalar_tensor_tensor(
+                    out=x1[:, j, :], in0=Y[g][j][:], scalar=c32[:, 2 * i : 2 * i + 1],
+                    in1=x_bf(i), op0=MULT, op1=ADD,
+                )
+            X1[g] = x1
+
+        def t1(g):
+            res = []
+            for j in range(2):
+                t = ps_t.tile([P, 4, P], F32, name="t1", tag="t1")
+                for q in range(4):
+                    nc.tensor.transpose(t[:, q, :], X1[g][:, j, q * P : (q + 1) * P], ident[:])
+                res.append(t)
+            T1[g] = res
+
+        def e1(g):
+            g1 = gpool.tile([P, 8 * P], BF16, name="g1", tag="g1", align_bytes=64)
+            for j in range(2):
+                nc.scalar.copy(
+                    out=g1[:, j * D : (j + 1) * D].rearrange("p (k t) -> p k t", t=4),
+                    in_=T1[g][j][:].rearrange("p t k -> p k t"),
+                )
+            G1[g] = g1
+
+        def a2(g):
+            o = opool.tile([P, 2, D], F32, name="o", tag="o")
+            for j in range(2):
+                i = 2 * g + j
+                nc.vector.scalar_tensor_tensor(
+                    out=o[:, j, :], in0=Z[g][j][:], scalar=c32[:, 2 * i + 1 : 2 * i + 2],
+                    in1=X1[g][:, j, :], op0=MULT, op1=ADD,
+                )
+            nc.sync.dma_start(
+                out=o_dram[:, 2 * g * D : (2 * g + 2) * D], in_=o[:].rearrange("p j d -> p (j d)")
+            )
+
+        def ok(g):
+            return 0 <= g < NP
+
+        for it in range(-1, NP + 3):
+            if ok(it + 1):
+                tx(it + 1)
+            if ok(it - 2):
+                t1(it - 2)
+            if ok(it + 1):
+                ex(it + 1)
+            if ok(it - 2):
+                e1(it - 2)
+            if ok(it + 1):
+                QX[it + 1] = quant(GX[it + 1], "cx", "sx")
+            if ok(it):
+                Y[it] = mm(ps_y, "y", QX[it], w0c, w0s)
+                a1(it)
+            if it == 0:
+                nc.vector.tensor_copy(out=w1g[:], in_=w1r[:].rearrange("p t n -> p n t"))
+            if it == 1:
+                nc.vector.quantize_mx(
+                    out=w1c[:].bitcast(FP8X4), scales=w1s[:],
+                    in_=w1g[:].rearrange("p n t -> p (n t)"),
+                )
+            if ok(it - 2):
+                Q1[it - 2] = quant(G1[it - 2], "c1", "s1")
+            if ok(it - 3):
+                Z[it - 3] = mm(ps_z, "z", Q1[it - 3], w1c, w1s)
+                a2(it - 3)

@@ -10,6 +10,7 @@ U8 = mybir.dt.uint8
 FP8X4 = mybir.dt.float8_e4m3fn_x4
 MULT = mybir.AluOpType.mult
 ADD = mybir.AluOpType.add
+COPY = mybir.ActivationFunctionType.Copy
 
 P = 128
 B = 8192
@@ -33,6 +34,7 @@ def tile_precomputedmetanet_pa_t_kernel(tc, transformed, coeff, task_mats, out):
         qpool = ctx.enter_context(tc.tile_pool(name="qpool", bufs=3))
         x1pool = ctx.enter_context(tc.tile_pool(name="x1pool", bufs=6))
         opool = ctx.enter_context(tc.tile_pool(name="opool", bufs=6))
+        czpool = ctx.enter_context(tc.tile_pool(name="czpool", bufs=3))
         ps_x = ctx.enter_context(tc.psum_pool(name="ps_x", bufs=2))
         ps_t = ctx.enter_context(tc.psum_pool(name="ps_t", bufs=2))
         ps_y = ctx.enter_context(tc.psum_pool(name="ps_y", bufs=2))
@@ -166,12 +168,17 @@ def tile_precomputedmetanet_pa_t_kernel(tc, transformed, coeff, task_mats, out):
 
         def a2(g):
             o = opool.tile([P, 2, D], F32, name="o", tag="o")
-            for j in range(2):
-                i = 2 * g + j
-                nc.vector.scalar_tensor_tensor(
-                    out=o[:, j, :], in0=Z[g][j][:], scalar=c32[:, 2 * i + 1 : 2 * i + 2],
-                    in1=X1[g][:, j, :], op0=MULT, op1=ADD,
-                )
+            i = 2 * g
+            nc.vector.scalar_tensor_tensor(
+                out=o[:, 0, :], in0=Z[g][0][:], scalar=c32[:, 2 * i + 1 : 2 * i + 2],
+                in1=X1[g][:, 0, :], op0=MULT, op1=ADD,
+            )
+            i = 2 * g + 1
+            cz = czpool.tile([P, D], F32, name="cz", tag="cz")
+            nc.scalar.activation(
+                out=cz[:], in_=Z[g][1][:], func=COPY, scale=c32[:, 2 * i + 1 : 2 * i + 2]
+            )
+            nc.gpsimd.tensor_tensor(out=o[:, 1, :], in0=cz[:], in1=X1[g][:, 1, :], op=ADD)
             nc.sync.dma_start(
                 out=o_dram[:, 2 * g * D : (2 * g + 2) * D], in_=o[:].rearrange("p j d -> p (j d)")
             )
@@ -190,6 +197,8 @@ def tile_precomputedmetanet_pa_t_kernel(tc, transformed, coeff, task_mats, out):
                 e1(it - 2)
             if ok(it + 1):
                 QX[it + 1] = quant(GX[it + 1], "cx", "sx")
+            if ok(it - 2):
+                Q1[it - 2] = quant(G1[it - 2], "c1", "s1")
             if ok(it):
                 Y[it] = mm(ps_y, "y", QX[it], w0c, w0s)
                 a1(it)
@@ -200,8 +209,6 @@ def tile_precomputedmetanet_pa_t_kernel(tc, transformed, coeff, task_mats, out):
                     out=w1c[:].bitcast(FP8X4), scales=w1s[:],
                     in_=w1g[:].rearrange("p n t -> p (n t)"),
                 )
-            if ok(it - 2):
-                Q1[it - 2] = quant(G1[it - 2], "c1", "s1")
             if ok(it - 3):
                 Z[it - 3] = mm(ps_z, "z", Q1[it - 3], w1c, w1s)
                 a2(it - 3)

@@ -63,7 +63,7 @@ def tile_precomputedmetanet_pa_t_kernel(tc, transformed, coeff, task_mats, out):
             start += n
             if c == 0:
                 nc.sync.dma_start(out=c_bf[:], in_=c_dram)
-            if c == 1:
+            if c == 2:
                 nc.sync.dma_start(out=w1r[:], in_=task_mats[1].rearrange("(t p) n -> p t n", t=4))
         assert start == NT
 
@@ -99,6 +99,8 @@ def tile_precomputedmetanet_pa_t_kernel(tc, transformed, coeff, task_mats, out):
         G1 = {}
         Q1 = {}
         Z = {}
+        O = {}
+        CZ = {}
 
         def tx(g):
             t = ps_x.tile([P, 2, 2, P], F32, name="tpx", tag="tpx")
@@ -122,9 +124,9 @@ def tile_precomputedmetanet_pa_t_kernel(tc, transformed, coeff, task_mats, out):
             return (cw, sc)
 
         def mm(pool, tag, q, wc, ws):
-            res = []
+            res = {}
             cw, sc = q
-            for j in range(2):
+            for j in (1, 0) if tag == "z" else (0, 1):
                 acc = pool.tile([P, D], F32, name=tag, tag=tag)
                 nc.tensor.matmul_mx(
                     out=acc[:],
@@ -135,18 +137,17 @@ def tile_precomputedmetanet_pa_t_kernel(tc, transformed, coeff, task_mats, out):
                     start=True,
                     stop=True,
                 )
-                res.append(acc)
+                res[j] = acc
             return res
 
-        def a1(g):
-            x1 = x1pool.tile([P, 2, D], F32, name="x1", tag="x1")
-            for j in range(2):
-                i = 2 * g + j
-                nc.vector.scalar_tensor_tensor(
-                    out=x1[:, j, :], in0=Y[g][j][:], scalar=c32[:, 2 * i : 2 * i + 1],
-                    in1=x_bf(i), op0=MULT, op1=ADD,
-                )
-            X1[g] = x1
+        def a1(g, j):
+            if j == 0:
+                X1[g] = x1pool.tile([P, 2, D], F32, name="x1", tag="x1")
+            i = 2 * g + j
+            nc.vector.scalar_tensor_tensor(
+                out=X1[g][:, j, :], in0=Y[g][j][:], scalar=c32[:, 2 * i : 2 * i + 1],
+                in1=x_bf(i), op0=MULT, op1=ADD,
+            )
 
         def t1(g):
             res = []
@@ -166,42 +167,60 @@ def tile_precomputedmetanet_pa_t_kernel(tc, transformed, coeff, task_mats, out):
                 )
             G1[g] = g1
 
-        def a2(g):
-            o = opool.tile([P, 2, D], F32, name="o", tag="o")
-            i = 2 * g
+        def a2v(g, j):
+            if j == 0:
+                O[g] = opool.tile([P, 2, D], F32, name="o", tag="o")
+            i = 2 * g + j
             nc.vector.scalar_tensor_tensor(
-                out=o[:, 0, :], in0=Z[g][0][:], scalar=c32[:, 2 * i + 1 : 2 * i + 2],
-                in1=X1[g][:, 0, :], op0=MULT, op1=ADD,
+                out=O[g][:, j, :], in0=Z[g][j][:], scalar=c32[:, 2 * i + 1 : 2 * i + 2],
+                in1=X1[g][:, j, :], op0=MULT, op1=ADD,
             )
+
+        def cz(g):
             i = 2 * g + 1
-            cz = czpool.tile([P, D], F32, name="cz", tag="cz")
+            t = czpool.tile([P, D], F32, name="cz", tag="cz")
             nc.scalar.activation(
-                out=cz[:], in_=Z[g][1][:], func=COPY, scale=c32[:, 2 * i + 1 : 2 * i + 2]
+                out=t[:], in_=Z[g][1][:], func=COPY, scale=c32[:, 2 * i + 1 : 2 * i + 2]
             )
-            nc.gpsimd.tensor_tensor(out=o[:, 1, :], in0=cz[:], in1=X1[g][:, 1, :], op=ADD)
+            CZ[g] = t
+
+        def ga(g):
+            nc.gpsimd.tensor_tensor(out=O[g][:, 1, :], in0=CZ[g][:], in1=X1[g][:, 1, :], op=ADD)
+
+        def store(g):
             nc.sync.dma_start(
-                out=o_dram[:, 2 * g * D : (2 * g + 2) * D], in_=o[:].rearrange("p j d -> p (j d)")
+                out=o_dram[:, 2 * g * D : (2 * g + 2) * D],
+                in_=O[g][:].rearrange("p j d -> p (j d)"),
             )
+
+        def off(g):
+            return g < NP - 1
 
         def ok(g):
             return 0 <= g < NP
 
-        for it in range(-1, NP + 3):
-            if ok(it + 1):
-                tx(it + 1)
+        for it in range(-2, NP + 3):
             if ok(it - 2):
                 t1(it - 2)
-            if ok(it + 1):
-                ex(it + 1)
-            if ok(it - 2):
                 e1(it - 2)
+            if ok(it):
+                Y[it] = mm(ps_y, "y", QX[it], w0c, w0s)
+            if ok(it - 3):
+                Z[it - 3] = mm(ps_z, "z", Q1[it - 3], w1c, w1s)
+            if ok(it + 2):
+                tx(it + 2)
+            if ok(it - 3) and off(it - 3):
+                cz(it - 3)
+            if ok(it + 2):
+                ex(it + 2)
+            if ok(it):
+                a1(it, 0)
             if ok(it + 1):
                 QX[it + 1] = quant(GX[it + 1], "cx", "sx")
             if ok(it - 2):
                 Q1[it - 2] = quant(G1[it - 2], "c1", "s1")
             if ok(it):
-                Y[it] = mm(ps_y, "y", QX[it], w0c, w0s)
-                a1(it)
+                a1(it, 1)
             if it == 0:
                 nc.vector.tensor_copy(out=w1g[:], in_=w1r[:].rearrange("p t n -> p n t"))
             if it == 1:
@@ -210,5 +229,9 @@ def tile_precomputedmetanet_pa_t_kernel(tc, transformed, coeff, task_mats, out):
                     in_=w1g[:].rearrange("p n t -> p (n t)"),
                 )
             if ok(it - 3):
-                Z[it - 3] = mm(ps_z, "z", Q1[it - 3], w1c, w1s)
-                a2(it - 3)
+                a2v(it - 3, 0)
+                if off(it - 3):
+                    ga(it - 3)
+                else:
+                    a2v(it - 3, 1)
+                store(it - 3)

@@ -20,6 +20,7 @@ NP = NT // 2
 FLOPS = 2 * 2 * B * D * D
 
 CHUNKS = [2, 2, 4, 8, 8, 8, 8, 8, 8, 8]
+W0_SPLIT = 384
 
 
 def tile_precomputedmetanet_pa_t_kernel(tc, transformed, coeff, task_mats, out):
@@ -63,7 +64,7 @@ def tile_precomputedmetanet_pa_t_kernel(tc, transformed, coeff, task_mats, out):
             start += n
             if c == 0:
                 nc.sync.dma_start(out=c_bf[:], in_=c_dram)
-            if c == 2:
+            if c == 1:
                 nc.sync.dma_start(out=w1r[:], in_=task_mats[1].rearrange("(t p) n -> p t n", t=4))
         assert start == NT
 
@@ -84,7 +85,14 @@ def tile_precomputedmetanet_pa_t_kernel(tc, transformed, coeff, task_mats, out):
         w1s = const.tile([P, D], U8, name="w1s", align_bytes=64)
         c32 = const.tile([P, 2 * NT], F32, name="c32")
 
-        nc.vector.tensor_copy(out=w0g[:], in_=w0r[:].rearrange("p t n -> p n t"))
+        nc.vector.tensor_copy(
+            out=w0g[:, 0:W0_SPLIT, :].rearrange("p (c i) t -> p c t i", i=4),
+            in_=w0r[:, :, 0:W0_SPLIT].rearrange("p t (c i) -> p c t i", i=4),
+        )
+        nc.scalar.copy(
+            out=w0g[:, W0_SPLIT:D, :].rearrange("p (c i) t -> p c t i", i=4),
+            in_=w0r[:, :, W0_SPLIT:D].rearrange("p t (c i) -> p c t i", i=4),
+        )
         nc.vector.tensor_copy(out=c32[:], in_=c_bf[:])
         nc.vector.quantize_mx(
             out=w0c[:].bitcast(FP8X4), scales=w0s[:], in_=w0g[:].rearrange("p n t -> p (n t)")
@@ -187,10 +195,10 @@ def tile_precomputedmetanet_pa_t_kernel(tc, transformed, coeff, task_mats, out):
         def ga(g):
             nc.gpsimd.tensor_tensor(out=O[g][:, 1, :], in0=CZ[g][:], in1=X1[g][:, 1, :], op=ADD)
 
-        def store(g):
+        def store(g, lo, hi):
             nc.sync.dma_start(
-                out=o_dram[:, 2 * g * D : (2 * g + 2) * D],
-                in_=O[g][:].rearrange("p j d -> p (j d)"),
+                out=o_dram[:, (2 * g + lo) * D : (2 * g + hi) * D],
+                in_=O[g][:, lo:hi, :].rearrange("p j d -> p (j d)"),
             )
 
         def off(g):
@@ -213,6 +221,12 @@ def tile_precomputedmetanet_pa_t_kernel(tc, transformed, coeff, task_mats, out):
                 cz(it - 3)
             if ok(it + 2):
                 ex(it + 2)
+            if it == -1 or it == 0:
+                h = (it + 1) * (D // 2)
+                nc.scalar.copy(
+                    out=w1g[:, h : h + D // 2, :].rearrange("p (c i) t -> p c t i", i=4),
+                    in_=w1r[:, :, h : h + D // 2].rearrange("p t (c i) -> p c t i", i=4),
+                )
             if ok(it):
                 a1(it, 0)
             if ok(it + 1):
@@ -221,8 +235,6 @@ def tile_precomputedmetanet_pa_t_kernel(tc, transformed, coeff, task_mats, out):
                 Q1[it - 2] = quant(G1[it - 2], "c1", "s1")
             if ok(it):
                 a1(it, 1)
-            if it == 0:
-                nc.vector.tensor_copy(out=w1g[:], in_=w1r[:].rearrange("p t n -> p n t"))
             if it == 1:
                 nc.vector.quantize_mx(
                     out=w1c[:].bitcast(FP8X4), scales=w1s[:],
@@ -232,6 +244,8 @@ def tile_precomputedmetanet_pa_t_kernel(tc, transformed, coeff, task_mats, out):
                 a2v(it - 3, 0)
                 if off(it - 3):
                     ga(it - 3)
+                    store(it - 3, 0, 2)
                 else:
+                    store(it - 3, 0, 1)
                     a2v(it - 3, 1)
-                store(it - 3)
+                    store(it - 3, 1, 2)

@@ -40,7 +40,6 @@ def tile_precomputedmetanet_pa_t_kernel(tc, transformed, coeff, task_mats, out):
         ps_t = ctx.enter_context(tc.psum_pool(name="ps_t", bufs=2))
         ps_y = ctx.enter_context(tc.psum_pool(name="ps_y", bufs=2))
         ps_z = ctx.enter_context(tc.psum_pool(name="ps_z", bufs=2))
-        ctx.enter_context(tc.manual_schedule())
 
         ident = const.tile([P, P], F32, name="ident")
         make_identity(nc, ident[:])

@@ -13,238 +13,261 @@ ADD = mybir.AluOpType.add
 COPY = mybir.ActivationFunctionType.Copy
 
 P = 128
-B = 8192
+PACK = 4
+TOKENS = 8192
 D = 512
-NT = B // P
-NP = NT // 2
-FLOPS = 2 * 2 * B * D * D
+N_TILES = TOKENS // P
+N_PAIRS = N_TILES // 2
+FLOPS = 2 * 2 * TOKENS * D * D
 
-CHUNKS = [2, 2, 4, 8, 8, 8, 8, 8, 8, 8]
-W0_SPLIT = 384
+LOAD_TILES = [2, 2, 4, 8, 8, 8, 8, 8, 8, 8]
+
+W0_VECTOR_COLS = 384
 
 
 def tile_precomputedmetanet_pa_t_kernel(tc, transformed, coeff, task_mats, out):
     nc = tc.nc
-    x_dram = transformed.rearrange("(p i) d -> p (i d)", i=NT)
-    o_dram = out.rearrange("(p i) d -> p (i d)", i=NT)
-    c_dram = coeff.rearrange("(p i) c -> p (i c)", i=NT)
+    x_dram = transformed.rearrange("(p i) d -> p (i d)", i=N_TILES)
+    out_dram = out.rearrange("(p i) d -> p (i d)", i=N_TILES)
+    coeff_dram = coeff.rearrange("(p i) c -> p (i c)", i=N_TILES)
 
     with ExitStack() as ctx:
         const = ctx.enter_context(tc.tile_pool(name="const", bufs=1))
-        gpool = ctx.enter_context(tc.tile_pool(name="gpool", bufs=3))
-        qpool = ctx.enter_context(tc.tile_pool(name="qpool", bufs=3))
-        x1pool = ctx.enter_context(tc.tile_pool(name="x1pool", bufs=6))
-        opool = ctx.enter_context(tc.tile_pool(name="opool", bufs=6))
-        czpool = ctx.enter_context(tc.tile_pool(name="czpool", bufs=3))
-        ps_x = ctx.enter_context(tc.psum_pool(name="ps_x", bufs=2))
-        ps_t = ctx.enter_context(tc.psum_pool(name="ps_t", bufs=2))
-        ps_y = ctx.enter_context(tc.psum_pool(name="ps_y", bufs=2))
-        ps_z = ctx.enter_context(tc.psum_pool(name="ps_z", bufs=2))
+        grouped_pool = ctx.enter_context(tc.tile_pool(name="gpool", bufs=3))
+        mx_pool = ctx.enter_context(tc.tile_pool(name="qpool", bufs=3))
+        x1_pool = ctx.enter_context(tc.tile_pool(name="x1pool", bufs=6))
+        out_pool = ctx.enter_context(tc.tile_pool(name="opool", bufs=6))
+        scaled_pool = ctx.enter_context(tc.tile_pool(name="czpool", bufs=3))
+        psum_transposed = ctx.enter_context(tc.psum_pool(name="ps_t", bufs=3))
+        psum_acc = ctx.enter_context(tc.psum_pool(name="ps_acc", bufs=5))
+        ctx.enter_context(tc.manual_schedule())
 
-        ident = const.tile([P, P], F32, name="ident")
-        make_identity(nc, ident[:])
+        identity = const.tile([P, P], F32, name="ident")
+        make_identity(nc, identity[:])
 
-        w0r = const.tile([P, 4, D], BF16, name="w0r")
+        w0_rows = const.tile([P, PACK, D], BF16, name="w0r")
         nc.sync.dma_start(
-            out=w0r[:].rearrange("p (u e) n -> p u (e n)", u=2),
-            in_=task_mats[0].rearrange("(u q e) n -> q u (e n)", u=2, e=2),
+            out=w0_rows[:].rearrange("p (u e) n -> p u (e n)", u=2),
+            in_=task_mats[0].rearrange("(u p e) n -> p u (e n)", u=2, e=2),
         )
-        xs = []
-        where = {}
-        start = 0
-        w1r = const.tile([P, 4, D], BF16, name="w1r")
-        c_bf = const.tile([P, 2 * NT], BF16, name="c_bf")
-        for c, n in enumerate(CHUNKS):
-            xc = const.tile([P, n * D], BF16, name="x%d" % c)
-            nc.sync.dma_start(out=xc[:], in_=x_dram[:, start * D : (start + n) * D])
-            xs.append(xc)
-            for k in range(n):
-                where[start + k] = (c, k)
-            start += n
-            if c == 0:
-                nc.sync.dma_start(out=c_bf[:], in_=c_dram)
-            if c == 1:
-                nc.sync.dma_start(out=w1r[:], in_=task_mats[1].rearrange("(t p) n -> p t n", t=4))
-        assert start == NT
+        w1_rows = const.tile([P, PACK, D], BF16, name="w1r")
+        coeff_bf16 = const.tile([P, 2 * N_TILES], BF16, name="c_bf")
+        x_loads = []
+        place = {}
+        first_tile = 0
+        for load, n_tiles in enumerate(LOAD_TILES):
+            x_load = const.tile([P, n_tiles * D], BF16, name="x%d" % load)
+            nc.sync.dma_start(
+                out=x_load[:], in_=x_dram[:, first_tile * D : (first_tile + n_tiles) * D]
+            )
+            x_loads.append(x_load)
+            for position in range(n_tiles):
+                place[first_tile + position] = (load, position)
+            first_tile += n_tiles
+            if load == 0:
+                nc.sync.dma_start(out=coeff_bf16[:], in_=coeff_dram)
+            if load == 1:
+                nc.sync.dma_start(
+                    out=w1_rows[:], in_=task_mats[1].rearrange("(t p) n -> p t n", t=PACK)
+                )
+        assert first_tile == N_TILES
 
-        def x_bf(i):
-            c, k = where[i]
-            return xs[c][:, k * D : (k + 1) * D]
+        def x_tile(i):
+            load, position = place[i]
+            return x_loads[load][:, position * D : (position + 1) * D]
 
-        def x_words(i, u):
-            c, k = where[i]
-            lo = k * (D // 2) + u * P
-            return xs[c][:].bitcast(F32)[:, lo : lo + P]
+        def x_tile_words(i, u):
+            load, position = place[i]
+            lo = position * (D // 2) + u * P
+            return x_loads[load][:].bitcast(F32)[:, lo : lo + P]
 
-        w0g = const.tile([P, D, 4], BF16, name="w0g", align_bytes=64)
-        w0c = const.tile([P, D], U32, name="w0c", align_bytes=64)
-        w0s = const.tile([P, D], U8, name="w0s", align_bytes=64)
-        w1g = const.tile([P, D, 4], BF16, name="w1g", align_bytes=64)
-        w1c = const.tile([P, D], U32, name="w1c", align_bytes=64)
-        w1s = const.tile([P, D], U8, name="w1s", align_bytes=64)
-        c32 = const.tile([P, 2 * NT], F32, name="c32")
+        w0_grouped = const.tile([P, D, PACK], BF16, name="w0g", align_bytes=64)
+        w0_codes = const.tile([P, D], U32, name="w0c", align_bytes=64)
+        w0_scales = const.tile([P, D], U8, name="w0s", align_bytes=64)
+        w1_grouped = const.tile([P, D, PACK], BF16, name="w1g", align_bytes=64)
+        w1_codes = const.tile([P, D], U32, name="w1c", align_bytes=64)
+        w1_scales = const.tile([P, D], U8, name="w1s", align_bytes=64)
+        coeff_f32 = const.tile([P, 2 * N_TILES], F32, name="c32")
 
-        nc.vector.tensor_copy(
-            out=w0g[:, 0:W0_SPLIT, :].rearrange("p (c i) t -> p c t i", i=4),
-            in_=w0r[:, :, 0:W0_SPLIT].rearrange("p t (c i) -> p c t i", i=4),
-        )
-        nc.scalar.copy(
-            out=w0g[:, W0_SPLIT:D, :].rearrange("p (c i) t -> p c t i", i=4),
-            in_=w0r[:, :, W0_SPLIT:D].rearrange("p t (c i) -> p c t i", i=4),
-        )
-        nc.vector.tensor_copy(out=c32[:], in_=c_bf[:])
-        nc.vector.quantize_mx(
-            out=w0c[:].bitcast(FP8X4), scales=w0s[:], in_=w0g[:].rearrange("p n t -> p (n t)")
-        )
+        def regroup(copy, grouped, rows, lo, hi):
+            copy(
+                out=grouped[:, lo:hi, :].rearrange("p (c r) t -> p c t r", r=4),
+                in_=rows[:, :, lo:hi].rearrange("p t (c r) -> p c t r", r=4),
+            )
 
-        TPX = {}
-        GX = {}
-        QX = {}
-        Y = {}
-        X1 = {}
-        T1 = {}
-        G1 = {}
-        Q1 = {}
-        Z = {}
-        O = {}
-        CZ = {}
+        def quantise_matrix(codes, scales, grouped):
+            nc.vector.quantize_mx(
+                out=codes[:].bitcast(FP8X4),
+                scales=scales[:],
+                in_=grouped[:].rearrange("p n t -> p (n t)"),
+            )
 
-        def tx(g):
-            t = ps_x.tile([P, 2, 2, P], F32, name="tpx", tag="tpx")
+        regroup(nc.vector.tensor_copy, w0_grouped, w0_rows, 0, W0_VECTOR_COLS)
+        regroup(nc.scalar.copy, w0_grouped, w0_rows, W0_VECTOR_COLS, D)
+        nc.vector.tensor_copy(out=coeff_f32[:], in_=coeff_bf16[:])
+        quantise_matrix(w0_codes, w0_scales, w0_grouped)
+
+        xt_bank = {}
+        xt_grouped = {}
+        xt_mx = {}
+        acc1 = {}
+        x1 = {}
+        x1t_banks = {}
+        x1t_grouped = {}
+        x1t_mx = {}
+        acc2 = {}
+        result = {}
+        scaled = {}
+
+        def transpose_x(pair):
+            bank = psum_transposed.tile([P, 2, 2, P], F32, name="tpx", tag="tp")
             for j in range(2):
                 for u in range(2):
-                    nc.tensor.transpose(t[:, j, u, :], x_words(2 * g + j, u), ident[:])
-            TPX[g] = t
+                    nc.tensor.transpose(
+                        bank[:, j, u, :], x_tile_words(2 * pair + j, u), identity[:]
+                    )
+            xt_bank[pair] = bank
 
-        def ex(g):
-            gx = gpool.tile([P, 8 * P], BF16, name="gx", tag="gx", align_bytes=64)
-            nc.scalar.copy(
-                out=gx[:].bitcast(F32).rearrange("p (j k u) -> p j k u", j=2, u=2),
-                in_=TPX[g][:].rearrange("p j u k -> p j k u"),
+        def copy_out_xt(pair):
+            grouped = grouped_pool.tile(
+                [P, 2 * P * PACK], BF16, name="gx", tag="gx", align_bytes=64
             )
-            GX[g] = gx
+            nc.scalar.copy(
+                out=grouped[:].bitcast(F32).rearrange("p (j m u) -> p j m u", j=2, u=2),
+                in_=xt_bank[pair][:].rearrange("p j u m -> p j m u"),
+            )
+            xt_grouped[pair] = grouped
 
-        def quant(src, tagc, tags):
-            cw = qpool.tile([P, 2 * P], U32, name=tagc, tag=tagc, align_bytes=64)
-            sc = qpool.tile([P, 2 * P], U8, name=tags, tag=tags, align_bytes=64)
-            nc.vector.quantize_mx(out=cw[:].bitcast(FP8X4), scales=sc[:], in_=src[:])
-            return (cw, sc)
+        def quantise_pair(grouped, codes_name, scales_name):
+            codes = mx_pool.tile([P, 2 * P], U32, name=codes_name, tag=codes_name, align_bytes=64)
+            scales = mx_pool.tile([P, 2 * P], U8, name=scales_name, tag=scales_name, align_bytes=64)
+            nc.vector.quantize_mx(out=codes[:].bitcast(FP8X4), scales=scales[:], in_=grouped[:])
+            return (codes, scales)
 
-        def mm(pool, tag, q, wc, ws):
-            res = {}
-            cw, sc = q
-            for j in (1, 0) if tag == "z" else (0, 1):
-                acc = pool.tile([P, D], F32, name=tag, tag=tag)
+        def matmul_pair(name, tokens_mx, w_codes, w_scales):
+            banks = []
+            codes, scales = tokens_mx
+            for j in range(2):
+                bank = psum_acc.tile([P, D], F32, name=name, tag="acc")
                 nc.tensor.matmul_mx(
-                    out=acc[:],
-                    lhsT=cw[:, j * P : (j + 1) * P].bitcast(FP8X4),
-                    lhsT_scale=sc[:, j * P : (j + 1) * P],
-                    rhs=wc[:].bitcast(FP8X4),
-                    rhs_scale=ws[:],
+                    out=bank[:],
+                    lhsT=codes[:, j * P : (j + 1) * P].bitcast(FP8X4),
+                    lhsT_scale=scales[:, j * P : (j + 1) * P],
+                    rhs=w_codes[:].bitcast(FP8X4),
+                    rhs_scale=w_scales[:],
                     start=True,
                     stop=True,
                 )
-                res[j] = acc
-            return res
+                banks.append(bank)
+            return banks
 
-        def a1(g, j):
+        def first_sum(pair, j):
             if j == 0:
-                X1[g] = x1pool.tile([P, 2, D], F32, name="x1", tag="x1")
-            i = 2 * g + j
+                x1[pair] = x1_pool.tile([P, 2, D], F32, name="x1", tag="x1")
+            i = 2 * pair + j
             nc.vector.scalar_tensor_tensor(
-                out=X1[g][:, j, :], in0=Y[g][j][:], scalar=c32[:, 2 * i : 2 * i + 1],
-                in1=x_bf(i), op0=MULT, op1=ADD,
+                out=x1[pair][:, j, :],
+                in0=acc1[pair][j][:],
+                scalar=coeff_f32[:, 2 * i : 2 * i + 1],
+                in1=x_tile(i),
+                op0=MULT,
+                op1=ADD,
             )
 
-        def t1(g):
-            res = []
+        def transpose_x1(pair):
+            banks = []
             for j in range(2):
-                t = ps_t.tile([P, 4, P], F32, name="t1", tag="t1")
-                for q in range(4):
-                    nc.tensor.transpose(t[:, q, :], X1[g][:, j, q * P : (q + 1) * P], ident[:])
-                res.append(t)
-            T1[g] = res
+                bank = psum_transposed.tile([P, PACK, P], F32, name="t1", tag="tp")
+                for t in range(PACK):
+                    nc.tensor.transpose(
+                        bank[:, t, :], x1[pair][:, j, t * P : (t + 1) * P], identity[:]
+                    )
+                banks.append(bank)
+            x1t_banks[pair] = banks
 
-        def e1(g):
-            g1 = gpool.tile([P, 8 * P], BF16, name="g1", tag="g1", align_bytes=64)
+        def copy_out_x1t(pair):
+            grouped = grouped_pool.tile(
+                [P, 2 * P * PACK], BF16, name="g1", tag="g1", align_bytes=64
+            )
             for j in range(2):
                 nc.scalar.copy(
-                    out=g1[:, j * D : (j + 1) * D].rearrange("p (k t) -> p k t", t=4),
-                    in_=T1[g][j][:].rearrange("p t k -> p k t"),
+                    out=grouped[:, j * D : (j + 1) * D].rearrange("p (m t) -> p m t", t=PACK),
+                    in_=x1t_banks[pair][j][:].rearrange("p t m -> p m t"),
                 )
-            G1[g] = g1
+            x1t_grouped[pair] = grouped
 
-        def a2v(g, j):
+        def second_sum_on_vector(pair, j):
             if j == 0:
-                O[g] = opool.tile([P, 2, D], F32, name="o", tag="o")
-            i = 2 * g + j
+                result[pair] = out_pool.tile([P, 2, D], F32, name="o", tag="o")
+            i = 2 * pair + j
             nc.vector.scalar_tensor_tensor(
-                out=O[g][:, j, :], in0=Z[g][j][:], scalar=c32[:, 2 * i + 1 : 2 * i + 2],
-                in1=X1[g][:, j, :], op0=MULT, op1=ADD,
+                out=result[pair][:, j, :],
+                in0=acc2[pair][j][:],
+                scalar=coeff_f32[:, 2 * i + 1 : 2 * i + 2],
+                in1=x1[pair][:, j, :],
+                op0=MULT,
+                op1=ADD,
             )
 
-        def cz(g):
-            i = 2 * g + 1
-            t = czpool.tile([P, D], F32, name="cz", tag="cz")
+        def scale_acc2_on_scalar(pair):
+            i = 2 * pair + 1
+            product = scaled_pool.tile([P, D], F32, name="cz", tag="cz")
             nc.scalar.activation(
-                out=t[:], in_=Z[g][1][:], func=COPY, scale=c32[:, 2 * i + 1 : 2 * i + 2]
+                out=product[:],
+                in_=acc2[pair][1][:],
+                func=COPY,
+                scale=coeff_f32[:, 2 * i + 1 : 2 * i + 2],
             )
-            CZ[g] = t
+            scaled[pair] = product
 
-        def ga(g):
-            nc.gpsimd.tensor_tensor(out=O[g][:, 1, :], in0=CZ[g][:], in1=X1[g][:, 1, :], op=ADD)
+        def add_x1_on_gpsimd(pair):
+            nc.gpsimd.tensor_tensor(
+                out=result[pair][:, 1, :], in0=scaled[pair][:], in1=x1[pair][:, 1, :], op=ADD
+            )
 
-        def store(g, lo, hi):
+        def store(pair, j_lo, j_hi):
             nc.sync.dma_start(
-                out=o_dram[:, (2 * g + lo) * D : (2 * g + hi) * D],
-                in_=O[g][:, lo:hi, :].rearrange("p j d -> p (j d)"),
+                out=out_dram[:, (2 * pair + j_lo) * D : (2 * pair + j_hi) * D],
+                in_=result[pair][:, j_lo:j_hi, :].rearrange("p j d -> p (j d)"),
             )
 
-        def off(g):
-            return g < NP - 1
+        def is_pair(pair):
+            return 0 <= pair < N_PAIRS
 
-        def ok(g):
-            return 0 <= g < NP
+        def splits_second_sum(pair):
+            return pair < N_PAIRS - 1
 
-        for it in range(-2, NP + 3):
-            if ok(it - 2):
-                t1(it - 2)
-                e1(it - 2)
-            if ok(it):
-                Y[it] = mm(ps_y, "y", QX[it], w0c, w0s)
-            if ok(it - 3):
-                Z[it - 3] = mm(ps_z, "z", Q1[it - 3], w1c, w1s)
-            if ok(it + 2):
-                tx(it + 2)
-            if ok(it - 3) and off(it - 3):
-                cz(it - 3)
-            if ok(it + 2):
-                ex(it + 2)
-            if it == -1 or it == 0:
-                h = (it + 1) * (D // 2)
-                nc.scalar.copy(
-                    out=w1g[:, h : h + D // 2, :].rearrange("p (c i) t -> p c t i", i=4),
-                    in_=w1r[:, :, h : h + D // 2].rearrange("p t (c i) -> p c t i", i=4),
-                )
-            if ok(it):
-                a1(it, 0)
-            if ok(it + 1):
-                QX[it + 1] = quant(GX[it + 1], "cx", "sx")
-            if ok(it - 2):
-                Q1[it - 2] = quant(G1[it - 2], "c1", "s1")
-            if ok(it):
-                a1(it, 1)
-            if it == 1:
-                nc.vector.quantize_mx(
-                    out=w1c[:].bitcast(FP8X4), scales=w1s[:],
-                    in_=w1g[:].rearrange("p n t -> p (n t)"),
-                )
-            if ok(it - 3):
-                a2v(it - 3, 0)
-                if off(it - 3):
-                    ga(it - 3)
+        for it in range(-1, N_PAIRS + 3):
+            if is_pair(it + 1):
+                transpose_x(it + 1)
+                copy_out_xt(it + 1)
+            if it == 0 or it == 1:
+                half = it * (D // 2)
+                regroup(nc.scalar.copy, w1_grouped, w1_rows, half, half + D // 2)
+            if is_pair(it - 2):
+                transpose_x1(it - 2)
+                copy_out_x1t(it - 2)
+            if is_pair(it - 3):
+                acc2[it - 3] = matmul_pair("z", x1t_mx[it - 3], w1_codes, w1_scales)
+                if splits_second_sum(it - 3):
+                    scale_acc2_on_scalar(it - 3)
+            if is_pair(it):
+                acc1[it] = matmul_pair("y", xt_mx[it], w0_codes, w0_scales)
+            if is_pair(it + 1):
+                xt_mx[it + 1] = quantise_pair(xt_grouped[it + 1], "cx", "sx")
+            if is_pair(it - 2):
+                x1t_mx[it - 2] = quantise_pair(x1t_grouped[it - 2], "c1", "s1")
+            if is_pair(it - 3):
+                second_sum_on_vector(it - 3, 0)
+                if splits_second_sum(it - 3):
+                    add_x1_on_gpsimd(it - 3)
                     store(it - 3, 0, 2)
                 else:
                     store(it - 3, 0, 1)
-                    a2v(it - 3, 1)
+                    second_sum_on_vector(it - 3, 1)
                     store(it - 3, 1, 2)
+            if is_pair(it):
+                first_sum(it, 0)
+                first_sum(it, 1)
+            if it == 1:
+                quantise_matrix(w1_codes, w1_scales, w1_grouped)

from contextlib import ExitStack

import concourse.mybir as mybir
from concourse.masks import make_identity

F32 = mybir.dt.float32
BF16 = mybir.dt.bfloat16
U32 = mybir.dt.uint32
U8 = mybir.dt.uint8
FP8X4 = mybir.dt.float8_e4m3fn_x4
MULT = mybir.AluOpType.mult
ADD = mybir.AluOpType.add
COPY = mybir.ActivationFunctionType.Copy

P = 128
PACK = 4
TOKENS = 8192
D = 512
N_TILES = TOKENS // P
N_PAIRS = N_TILES // 2
FLOPS = 2 * 2 * TOKENS * D * D

LOAD_TILES = [2, 2, 4, 8, 8, 8, 8, 8, 8, 8]

W0_VECTOR_COLS = 384


def tile_precomputedmetanet_pa_t_kernel(tc, transformed, coeff, task_mats, out):
    nc = tc.nc
    x_dram = transformed.rearrange("(p i) d -> p (i d)", i=N_TILES)
    out_dram = out.rearrange("(p i) d -> p (i d)", i=N_TILES)
    coeff_dram = coeff.rearrange("(p i) c -> p (i c)", i=N_TILES)

    with ExitStack() as ctx:
        const = ctx.enter_context(tc.tile_pool(name="const", bufs=1))
        grouped_pool = ctx.enter_context(tc.tile_pool(name="gpool", bufs=3))
        mx_pool = ctx.enter_context(tc.tile_pool(name="qpool", bufs=3))
        x1_pool = ctx.enter_context(tc.tile_pool(name="x1pool", bufs=6))
        out_pool = ctx.enter_context(tc.tile_pool(name="opool", bufs=6))
        scaled_pool = ctx.enter_context(tc.tile_pool(name="czpool", bufs=3))
        psum_transposed = ctx.enter_context(tc.psum_pool(name="ps_t", bufs=3))
        psum_acc = ctx.enter_context(tc.psum_pool(name="ps_acc", bufs=5))
        ctx.enter_context(tc.manual_schedule())

        identity = const.tile([P, P], F32, name="ident")
        make_identity(nc, identity[:])

        w0_rows = const.tile([P, PACK, D], BF16, name="w0r")
        nc.sync.dma_start(
            out=w0_rows[:].rearrange("p (u e) n -> p u (e n)", u=2),
            in_=task_mats[0].rearrange("(u p e) n -> p u (e n)", u=2, e=2),
        )
        w1_rows = const.tile([P, PACK, D], BF16, name="w1r")
        coeff_bf16 = const.tile([P, 2 * N_TILES], BF16, name="c_bf")
        x_loads = []
        place = {}
        first_tile = 0
        for load, n_tiles in enumerate(LOAD_TILES):
            x_load = const.tile([P, n_tiles * D], BF16, name="x%d" % load)
            nc.sync.dma_start(
                out=x_load[:], in_=x_dram[:, first_tile * D : (first_tile + n_tiles) * D]
            )
            x_loads.append(x_load)
            for position in range(n_tiles):
                place[first_tile + position] = (load, position)
            first_tile += n_tiles
            if load == 0:
                nc.sync.dma_start(out=coeff_bf16[:], in_=coeff_dram)
            if load == 1:
                nc.sync.dma_start(
                    out=w1_rows[:], in_=task_mats[1].rearrange("(t p) n -> p t n", t=PACK)
                )
        assert first_tile == N_TILES

        def x_tile(i):
            load, position = place[i]
            return x_loads[load][:, position * D : (position + 1) * D]

        def x_tile_words(i, u):
            load, position = place[i]
            lo = position * (D // 2) + u * P
            return x_loads[load][:].bitcast(F32)[:, lo : lo + P]

        w0_grouped = const.tile([P, D, PACK], BF16, name="w0g", align_bytes=64)
        w0_codes = const.tile([P, D], U32, name="w0c", align_bytes=64)
        w0_scales = const.tile([P, D], U8, name="w0s", align_bytes=64)
        w1_grouped = const.tile([P, D, PACK], BF16, name="w1g", align_bytes=64)
        w1_codes = const.tile([P, D], U32, name="w1c", align_bytes=64)
        w1_scales = const.tile([P, D], U8, name="w1s", align_bytes=64)
        coeff_f32 = const.tile([P, 2 * N_TILES], F32, name="c32")

        def regroup(copy, grouped, rows, lo, hi):
            copy(
                out=grouped[:, lo:hi, :].rearrange("p (c r) t -> p c t r", r=4),
                in_=rows[:, :, lo:hi].rearrange("p t (c r) -> p c t r", r=4),
            )

        def quantise_matrix(codes, scales, grouped):
            nc.vector.quantize_mx(
                out=codes[:].bitcast(FP8X4),
                scales=scales[:],
                in_=grouped[:].rearrange("p n t -> p (n t)"),
            )

        regroup(nc.vector.tensor_copy, w0_grouped, w0_rows, 0, W0_VECTOR_COLS)
        regroup(nc.scalar.copy, w0_grouped, w0_rows, W0_VECTOR_COLS, D)
        nc.vector.tensor_copy(out=coeff_f32[:], in_=coeff_bf16[:])
        quantise_matrix(w0_codes, w0_scales, w0_grouped)

        xt_bank = {}
        xt_grouped = {}
        xt_mx = {}
        acc1 = {}
        x1 = {}
        x1t_banks = {}
        x1t_grouped = {}
        x1t_mx = {}
        acc2 = {}
        result = {}
        scaled = {}

        def transpose_x(pair):
            bank = psum_transposed.tile([P, 2, 2, P], F32, name="tpx", tag="tp")
            for j in range(2):
                for u in range(2):
                    nc.tensor.transpose(
                        bank[:, j, u, :], x_tile_words(2 * pair + j, u), identity[:]
                    )
            xt_bank[pair] = bank

        def copy_out_xt(pair):
            grouped = grouped_pool.tile(
                [P, 2 * P * PACK], BF16, name="gx", tag="gx", align_bytes=64
            )
            nc.scalar.copy(
                out=grouped[:].bitcast(F32).rearrange("p (j m u) -> p j m u", j=2, u=2),
                in_=xt_bank[pair][:].rearrange("p j u m -> p j m u"),
            )
            xt_grouped[pair] = grouped

        def quantise_pair(grouped, codes_name, scales_name):
            codes = mx_pool.tile([P, 2 * P], U32, name=codes_name, tag=codes_name, align_bytes=64)
            scales = mx_pool.tile([P, 2 * P], U8, name=scales_name, tag=scales_name, align_bytes=64)
            nc.vector.quantize_mx(out=codes[:].bitcast(FP8X4), scales=scales[:], in_=grouped[:])
            return (codes, scales)

        def matmul_pair(name, tokens_mx, w_codes, w_scales):
            banks = []
            codes, scales = tokens_mx
            for j in range(2):
                bank = psum_acc.tile([P, D], F32, name=name, tag="acc")
                nc.tensor.matmul_mx(
                    out=bank[:],
                    lhsT=codes[:, j * P : (j + 1) * P].bitcast(FP8X4),
                    lhsT_scale=scales[:, j * P : (j + 1) * P],
                    rhs=w_codes[:].bitcast(FP8X4),
                    rhs_scale=w_scales[:],
                    start=True,
                    stop=True,
                )
                banks.append(bank)
            return banks

        def first_sum(pair, j):
            if j == 0:
                x1[pair] = x1_pool.tile([P, 2, D], F32, name="x1", tag="x1")
            i = 2 * pair + j
            nc.vector.scalar_tensor_tensor(
                out=x1[pair][:, j, :],
                in0=acc1[pair][j][:],
                scalar=coeff_f32[:, 2 * i : 2 * i + 1],
                in1=x_tile(i),
                op0=MULT,
                op1=ADD,
            )

        def transpose_x1(pair):
            banks = []
            for j in range(2):
                bank = psum_transposed.tile([P, PACK, P], F32, name="t1", tag="tp")
                for t in range(PACK):
                    nc.tensor.transpose(
                        bank[:, t, :], x1[pair][:, j, t * P : (t + 1) * P], identity[:]
                    )
                banks.append(bank)
            x1t_banks[pair] = banks

        def copy_out_x1t(pair):
            grouped = grouped_pool.tile(
                [P, 2 * P * PACK], BF16, name="g1", tag="g1", align_bytes=64
            )
            for j in range(2):
                nc.scalar.copy(
                    out=grouped[:, j * D : (j + 1) * D].rearrange("p (m t) -> p m t", t=PACK),
                    in_=x1t_banks[pair][j][:].rearrange("p t m -> p m t"),
                )
            x1t_grouped[pair] = grouped

        def second_sum_on_vector(pair, j):
            if j == 0:
                result[pair] = out_pool.tile([P, 2, D], F32, name="o", tag="o")
            i = 2 * pair + j
            nc.vector.scalar_tensor_tensor(
                out=result[pair][:, j, :],
                in0=acc2[pair][j][:],
                scalar=coeff_f32[:, 2 * i + 1 : 2 * i + 2],
                in1=x1[pair][:, j, :],
                op0=MULT,
                op1=ADD,
            )

        def scale_acc2_on_scalar(pair):
            i = 2 * pair + 1
            product = scaled_pool.tile([P, D], F32, name="cz", tag="cz")
            nc.scalar.activation(
                out=product[:],
                in_=acc2[pair][1][:],
                func=COPY,
                scale=coeff_f32[:, 2 * i + 1 : 2 * i + 2],
            )
            scaled[pair] = product

        def add_x1_on_gpsimd(pair):
            nc.gpsimd.tensor_tensor(
                out=result[pair][:, 1, :], in0=scaled[pair][:], in1=x1[pair][:, 1, :], op=ADD
            )

        def store(pair, j_lo, j_hi):
            nc.sync.dma_start(
                out=out_dram[:, (2 * pair + j_lo) * D : (2 * pair + j_hi) * D],
                in_=result[pair][:, j_lo:j_hi, :].rearrange("p j d -> p (j d)"),
            )

        def is_pair(pair):
            return 0 <= pair < N_PAIRS

        def splits_second_sum(pair):
            return pair < N_PAIRS - 1

        for it in range(-1, N_PAIRS + 3):
            if is_pair(it + 1):
                transpose_x(it + 1)
                copy_out_xt(it + 1)
            if it == 0 or it == 1:
                half = it * (D // 2)
                regroup(nc.scalar.copy, w1_grouped, w1_rows, half, half + D // 2)
            if is_pair(it - 2):
                transpose_x1(it - 2)
                copy_out_x1t(it - 2)
            if is_pair(it - 3):
                acc2[it - 3] = matmul_pair("z", x1t_mx[it - 3], w1_codes, w1_scales)
                if splits_second_sum(it - 3):
                    scale_acc2_on_scalar(it - 3)
            if is_pair(it):
                acc1[it] = matmul_pair("y", xt_mx[it], w0_codes, w0_scales)
            if is_pair(it + 1):
                xt_mx[it + 1] = quantise_pair(xt_grouped[it + 1], "cx", "sx")
            if is_pair(it - 2):
                x1t_mx[it - 2] = quantise_pair(x1t_grouped[it - 2], "c1", "s1")
            if is_pair(it - 3):
                second_sum_on_vector(it - 3, 0)
                if splits_second_sum(it - 3):
                    add_x1_on_gpsimd(it - 3)
                    store(it - 3, 0, 2)
                else:
                    store(it - 3, 0, 1)
                    second_sum_on_vector(it - 3, 1)
                    store(it - 3, 1, 2)
            if is_pair(it):
                first_sum(it, 0)
                first_sum(it, 1)
            if it == 1:
                quantise_matrix(w1_codes, w1_scales, w1_grouped)
